import numpy as np
import ml_dtypes


def mxq(x, axis, fmt="e4m3"):
    dtype, down = {"e4m3": (ml_dtypes.float8_e4m3fn, 7), "e5m2": (ml_dtypes.float8_e5m2, 14)}[fmt]
    v = np.moveaxis(np.asarray(x, np.float32).astype(ml_dtypes.bfloat16).astype(np.float64), axis, -1)
    blocks = v.reshape(v.shape[:-1] + (-1, 32))
    amax = np.abs(blocks).max(-1, keepdims=True)
    byte = np.maximum(np.where(amax > 0, np.frexp(amax)[1] - 1 + 127, 0) - down, 1)
    scale = np.exp2(byte - 127.0)
    codes = (blocks / scale).astype(np.float32).astype(dtype).astype(np.float64)
    return np.moveaxis((codes * scale).reshape(v.shape), -1, axis)


WIDE = False


def mx_kscale(k):
    if not WIDE:
        return np.ones(k)
    levels = np.array([10, -10, 5, -5, 0])
    a = np.random.permutation(np.resize(levels, k // 512 * 4)).reshape(k // 512, 4)
    idx = np.arange(k)
    return np.exp2(a[idx // 512, idx % 128 // 32])


BF16 = ml_dtypes.bfloat16


def bf(x):
    return np.asarray(x, np.float32).astype(BF16)


def f64(x):
    return np.asarray(x).astype(np.float64)


B, T, E, Q = 4, 512, 1024, 512
EPS_RMS = 1.1920929e-07


def silu(t):
    return t * (1.0 / (1.0 + np.exp(-t)))


def rms_norm(t):
    return t * (1.0 / np.sqrt(np.mean(t * t, axis=-1, keepdims=True) + EPS_RMS))


def w_norm(w, n):
    target_std = n ** (-0.5)
    return w * (target_std / (np.std(w, ddof=1) + 1e-08))


def setup_inputs():
    s = mx_kscale(E)
    u = s / s.min()
    row = np.where(u > 1.0, np.sqrt(EPS_RMS) / u, np.sqrt(T / (B * E)) * np.exp2(np.random.uniform(-1.0, 1.0, E)))
    return {"ao": bf(np.random.standard_normal((E, E)) * row[:, None]),
            "w_qkv": bf(np.random.standard_normal((3 * Q, E)) / np.sqrt(E) * u),
            "out_w": bf((np.random.standard_normal((E, E)) * np.sqrt(E) + 2.0) / E * u[:, None]),
            "tao": bf(np.random.uniform(0.5, 1.5, 1) * np.random.choice([-1.0, 1.0], 1))}


def reference(ao, w_qkv, out_w, tao):
    w = f64(w_qkv)
    alpha = np.clip(np.abs(f64(tao)), 1e-08, 1.0)
    ao_n = rms_norm(f64(ao))
    n1 = silu(mxq(w, 1, "e4m3") @ mxq(ao_n, 0, "e4m3"))
    upd = mxq(n1, 1, "e4m3") @ mxq(f64(out_w).T, 0, "e4m3")
    return w_norm(w + upd, E) * alpha

@@ -1,0 +1,299 @@
+from contextlib import ExitStack
+
+import concourse.mybir as mybir
+from concourse.masks import make_identity
+
+F32 = mybir.dt.float32
+BF16 = mybir.dt.bfloat16
+U32 = mybir.dt.uint32
+U8 = mybir.dt.uint8
+FP8X4 = mybir.dt.float8_e4m3fn_x4
+ALU = mybir.AluOpType
+ACT = mybir.ActivationFunctionType
+AX = mybir.AxisListType
+
+P = 128
+E = 1024
+R = 1536
+RT = R // P
+FT = E // P
+EPS_RMS = 1.1920929e-07
+COUNT = R * E
+LEAD = 8
+
+FLOPS = 2 * 2 * R * E * E
+
+
+def tile_retentionmechanism_pb_kernel(tc, ao, w_qkv, out_w, tao, out):
+    nc = tc.nc
+    with ExitStack() as ctx:
+        keep = ctx.enter_context(tc.tile_pool(name="keep", bufs=1))
+        big = ctx.enter_context(tc.tile_pool(name="big", bufs=1))
+        swap = ctx.enter_context(tc.tile_pool(name="swap", bufs=1))
+        psum = ctx.enter_context(tc.psum_pool(name="psum", bufs=8))
+        ctx.enter_context(tc.manual_schedule())
+
+        ident = keep.tile([P, P], F32)
+        make_identity(nc, ident[:])
+        neg_half = keep.tile([P, 4], F32)
+        nc.gpsimd.memset(neg_half[:], -0.5)
+        half = keep.tile([P, 1], F32)
+        nc.gpsimd.memset(half[:], 0.5)
+        ones = keep.tile([P, P], F32)
+        nc.vector.memset(ones[:], 1.0)
+        warm = keep.tile([P, 1], F32)
+        nc.vector.memset(warm[:], 0.0)
+
+        tao_sb = keep.tile([P, 1], BF16)
+        nc.scalar.dma_start(out=tao_sb[:], in_=tao.partition_broadcast(P))
+        warm_out = keep.tile([P, 1], F32)
+        nc.scalar.activation(out=warm_out[:], in_=warm[:], func=ACT.Silu)
+
+        ao_sb = swap.tile([P, 2, 2, 2, E], BF16, tag="swap", align_bytes=64)
+        ao_v = ao.rearrange("(c u p q) e -> c u p (q e)", c=2, u=2, q=2)
+        for c in range(2):
+            for u in range(2):
+                nc.sync.dma_start(out=ao_sb[:, c, u].rearrange("p q e -> p (q e)"), in_=ao_v[c, u])
+        w_sb = keep.tile([P, RT, E], BF16)
+        w_v = w_qkv.rearrange("(p i) d -> p i d", i=RT)
+        for i in range(0, RT, 2):
+            nc.sync.dma_start(out=w_sb[:, i : i + 2, :], in_=w_v[:, i : i + 2, :])
+        ow_sb = keep.tile([P, FT, E], BF16)
+        ow_v = out_w.rearrange("(h p) e -> p h e", p=P)
+        nc.sync.dma_start(out=ow_sb[:, 0:4, :], in_=ow_v[:, 0:4, :])
+        nc.sync.dma_start(out=ow_sb[:, 4:8, :], in_=ow_v[:, 4:8, :])
+
+        early = big.tile([P, (RT + 8) * E], BF16, tag="big", align_bytes=64)
+        w_grouped = early[:, 0 : RT * E].rearrange("p (i x) -> p i x", i=RT)
+        a_grouped = early[:, RT * E : (RT + 8) * E].rearrange("p (g c w j) -> p g c w j", g=2, c=2, j=4)
+        a_codes = keep.tile([P, 2, 2, 512], U32, align_bytes=64)
+        a_scales = keep.tile([P, 2, 2, 512], U8, align_bytes=64)
+        w_codes = keep.tile([P, RT, 2, P], U32, align_bytes=64)
+        w_scales = keep.tile([P, RT, 2, P], U8, align_bytes=64)
+        o_codes = keep.tile([P, 2, E], U32, align_bytes=64)
+        o_scales = keep.tile([P, 2, E], U8, align_bytes=64)
+        n_grouped = keep.tile([P, RT, 2, P, 4], BF16, align_bytes=64)
+        n_codes = keep.tile([P, RT, 2, P], U32, align_bytes=64)
+        n_scales = keep.tile([P, RT, 2, P], U8, align_bytes=64)
+        junk_v = keep.tile([P, E], BF16)
+        junk_s = keep.tile([P, E], BF16)
+        ss_v = keep.tile([P, 2, 2], F32)
+        ss_s = keep.tile([P, 2, 2], F32)
+        ms = keep.tile([P, 2, 2, 2], F32)
+        rstd = keep.tile([P, 2, 4], F32)
+        s1 = keep.tile([P, 2 * RT], F32)
+        s2 = keep.tile([P, 2 * RT], F32)
+        w_words = w_sb[:].bitcast(F32)
+        o_words = ow_sb[:].bitcast(F32)
+
+        def sum_squares(c, u):
+            nc.vector.scalar_tensor_tensor(
+                out=junk_v[:], in0=ao_sb[:, c, u, 0, :], scalar=1.0, in1=ao_sb[:, c, u, 0, :],
+                op0=ALU.mult, op1=ALU.mult, accum_out=ss_v[:, c, u : u + 1],
+            )
+            nc.scalar.activation(out=junk_s[:], in_=ao_sb[:, c, u, 1, :], func=ACT.Square, accum_out=ss_s[:, c, u : u + 1])
+
+        def inverse_rms(c):
+            nc.vector.tensor_scalar(out=ms[:, c, :, 0], in0=ss_v[:, c, :], scalar1=1.0 / E, scalar2=EPS_RMS, op0=ALU.mult, op1=ALU.add)
+            nc.vector.tensor_scalar(out=ms[:, c, :, 1], in0=ss_s[:, c, :], scalar1=1.0 / E, scalar2=EPS_RMS, op0=ALU.mult, op1=ALU.add)
+            nc.gpsimd.tensor_tensor(out=rstd[:, c, :], in0=ms[:, c].rearrange("p u q -> p (u q)"), in1=neg_half[:], op=ALU.pow)
+
+        def scale_a(c, g):
+            for j in range(4):
+                part = ao_sb[:, c, j // 2, j % 2, 512 * g : 512 * (g + 1)]
+                nc.vector.tensor_scalar(out=part, in0=part, scalar1=rstd[:, c, j : j + 1], scalar2=None, op0=ALU.mult)
+
+        def regroup_a(g, c):
+            src = ao_sb[:, c].rearrange("p u q e -> p (u q) e")[:, :, 512 * g : 512 * (g + 1)]
+            nc.vector.tensor_copy(
+                out=a_grouped[:, g, c].rearrange("p (v s m) j -> p v s m j", v=2, s=2),
+                in_=src.rearrange("p j (v m s) -> p v s m j", v=2, s=2),
+            )
+
+        def quantise_a(g):
+            nc.vector.quantize_mx(
+                out=a_codes[:, g].rearrange("p c w -> p (c w)").bitcast(FP8X4),
+                scales=a_scales[:, g].rearrange("p c w -> p (c w)"),
+                in_=a_grouped[:, g].rearrange("p c w j -> p (c w j)"),
+            )
+
+        def transpose_w(i):
+            xt = psum.tile([P, 4, P], F32, tag="bank", name="xt")
+            for b in range(4):
+                nc.tensor.transpose(xt[:, b, :], w_words[:, i, P * b : P * (b + 1)], ident[:])
+            nc.scalar.copy(
+                out=w_grouped[:, i, :].bitcast(F32).rearrange("p (c r u) -> p c r u", c=2, u=2),
+                in_=xt[:].rearrange("p (c u) r -> p c r u", c=2),
+            )
+
+        def quantise_w(i):
+            nc.vector.quantize_mx(
+                out=w_codes[:, i].rearrange("p c r -> p (c r)").bitcast(FP8X4),
+                scales=w_scales[:, i].rearrange("p c r -> p (c r)"),
+                in_=w_grouped[:, i, :],
+            )
+
+        def multiply_one(i, g):
+            acc = psum.tile([P, 4, P], F32, tag="bank", name="acc1")
+            for t in range(4):
+                for c in range(2):
+                    nc.tensor.matmul_mx(
+                        out=acc[:, t, :],
+                        lhsT=a_codes[:, g, c, P * t : P * (t + 1)].bitcast(FP8X4),
+                        lhsT_scale=a_scales[:, g, c, P * t : P * (t + 1)],
+                        rhs=w_codes[:, i, c, :].bitcast(FP8X4),
+                        rhs_scale=w_scales[:, i, c, :],
+                        start=(c == 0),
+                        stop=(c == 1),
+                    )
+            nc.scalar.activation(out=n_grouped[:, i, g], in_=acc[:].rearrange("p t r -> p r t"), func=ACT.Silu)
+
+        def quantise_n(i):
+            nc.vector.quantize_mx(
+                out=n_codes[:, i].rearrange("p g r -> p (g r)").bitcast(FP8X4),
+                scales=n_scales[:, i].rearrange("p g r -> p (g r)"),
+                in_=n_grouped[:, i].rearrange("p g r t -> p (g r t)"),
+            )
+
+        for c in range(2):
+            for u in range(2):
+                sum_squares(c, u)
+            inverse_rms(c)
+        for i in range(RT):
+            transpose_w(i)
+        scale_a(0, 0)
+        regroup_a(0, 0)
+        scale_a(1, 0)
+        regroup_a(0, 1)
+        quantise_w(0)
+        quantise_a(0)
+        for i in range(1, LEAD):
+            quantise_w(i)
+
+        tneg = keep.tile([P, 1], F32)
+        nc.vector.tensor_scalar(out=tneg[:], in0=tao_sb[:], scalar1=-1.0, scalar2=None, op0=ALU.mult)
+        tabs = keep.tile([P, 1], F32)
+        nc.vector.tensor_tensor(out=tabs[:], in0=tneg[:], in1=tao_sb[:], op=ALU.max)
+        tclip = keep.tile([P, 1], F32)
+        nc.vector.tensor_scalar(out=tclip[:], in0=tabs[:], scalar1=1e-08, scalar2=1.0, op0=ALU.max, op1=ALU.min)
+        gate = keep.tile([P, 1], F32)
+        nc.vector.tensor_scalar(out=gate[:], in0=tclip[:], scalar1=1.0 / 32.0, scalar2=None, op0=ALU.mult)
+
+        scale_a(0, 1)
+        regroup_a(1, 0)
+        scale_a(1, 1)
+        regroup_a(1, 1)
+        quantise_a(1)
+
+        for i in range(LEAD):
+            multiply_one(i, 0)
+
+        o_grouped = swap.tile([P, 2, 4 * E], BF16, tag="swap", align_bytes=64)
+        o_grouped_words = o_grouped[:].bitcast(F32).rearrange("p g (f v) -> p g f v", v=2)
+        for h in range(FT):
+            xt = psum.tile([P, 4, P], F32, tag="bank", name="xt")
+            for b in range(4):
+                nc.tensor.transpose(xt[:, b, :], o_words[:, h, P * b : P * (b + 1)], ident[:])
+            src = xt[:].rearrange("p (g v) f -> p g f v", g=2)
+            dst = o_grouped_words[:, :, P * h : P * (h + 1), :]
+            if h % 2 == 0:
+                nc.vector.tensor_copy(out=dst, in_=src)
+            else:
+                nc.scalar.copy(out=dst, in_=src)
+
+        def quantise_o(g, fh):
+            nc.vector.quantize_mx(
+                out=o_codes[:, g, 512 * fh : 512 * (fh + 1)].bitcast(FP8X4),
+                scales=o_scales[:, g, 512 * fh : 512 * (fh + 1)],
+                in_=o_grouped[:, g, 2048 * fh : 2048 * (fh + 1)],
+            )
+
+        for i in range(LEAD):
+            multiply_one(i, 1)
+        quantise_w(8)
+        quantise_o(0, 0)
+        quantise_o(1, 0)
+        quantise_n(0)
+        quantise_o(0, 1)
+        quantise_o(1, 1)
+        quantise_n(1)
+        for k in range(3):
+            quantise_w(9 + k)
+            quantise_n(2 + 2 * k)
+            quantise_n(3 + 2 * k)
+
+        z = big.tile([P, RT, E], F32, tag="big", align_bytes=64)
+
+        def multiply_two(k):
+            i, fh = k // 2, k % 2
+            cols = slice(512 * fh, 512 * (fh + 1))
+            acc = psum.tile([P, 512], F32, tag="bank", name="acc2")
+            for g in range(2):
+                nc.tensor.matmul_mx(
+                    out=acc[:],
+                    lhsT=n_codes[:, i, g, :].bitcast(FP8X4),
+                    lhsT_scale=n_scales[:, i, g, :],
+                    rhs=o_codes[:, g, cols].bitcast(FP8X4),
+                    rhs_scale=o_scales[:, g, cols],
+                    start=(g == 0),
+                    stop=(g == 1),
+                )
+            nc.vector.scalar_tensor_tensor(
+                out=z[:, i, cols], in0=acc[:], scalar=1.0, in1=w_sb[:, i, cols],
+                op0=ALU.mult, op1=ALU.add, accum_out=s1[:, k : k + 1],
+            )
+
+        def square_sum(k):
+            i, fh = k // 2, k % 2
+            nc.scalar.activation(
+                out=junk_s[:, 0:512], in_=z[:, i, 512 * fh : 512 * (fh + 1)], func=ACT.Square, accum_out=s2[:, k : k + 1]
+            )
+
+        squared = 0
+        for k in range(RT - LEAD):
+            multiply_one(LEAD + k, 0)
+            multiply_one(LEAD + k, 1)
+            for unit in range(4 * k, 4 * k + 4):
+                multiply_two(unit)
+            quantise_n(LEAD + k)
+            while squared < 4 * k + 3:
+                square_sum(squared)
+                squared += 1
+        for unit in range(4 * (RT - LEAD), 2 * RT):
+            multiply_two(unit)
+            square_sum(squared)
+            squared += 1
+        while squared < 2 * RT:
+            square_sum(squared)
+            squared += 1
+
+        tot_ps = psum.tile([P, 2, 2 * RT], F32, tag="bank", name="tot_ps")
+        nc.tensor.matmul(out=tot_ps[:, 0, :], lhsT=ones[:], rhs=s1[:], start=True, stop=True)
+        nc.tensor.matmul(out=tot_ps[:, 1, :], lhsT=ones[:], rhs=s2[:], start=True, stop=True)
+        tot = keep.tile([P, 2], F32)
+        nc.vector.tensor_reduce(out=tot[:], in_=tot_ps[:], axis=AX.X, op=ALU.add)
+        msq = keep.tile([P, 1], F32)
+        nc.vector.scalar_tensor_tensor(
+            out=msq[:], in0=tot[:, 0:1], scalar=-1.0 / COUNT, in1=tot[:, 0:1], op0=ALU.mult, op1=ALU.mult
+        )
+        dev = keep.tile([P, 1], F32)
+        nc.vector.tensor_scalar(out=dev[:], in0=msq[:], scalar1=tot[:, 1:2], scalar2=0.0, op0=ALU.add, op1=ALU.max)
+        root = keep.tile([P, 1], F32)
+        nc.gpsimd.tensor_tensor(out=root[:], in0=dev[:], in1=half[:], op=ALU.pow)
+        den = keep.tile([P, 1], F32)
+        nc.vector.tensor_scalar(
+            out=den[:], in0=root[:], scalar1=(COUNT - 1.0) ** -0.5, scalar2=1e-08, op0=ALU.mult, op1=ALU.add
+        )
+        inv = keep.tile([P, 1], F32)
+        nc.vector.reciprocal(out=inv[:], in_=den[:])
+        factor = keep.tile([P, 1], F32)
+        nc.vector.tensor_tensor(out=factor[:], in0=inv[:], in1=gate[:], op=ALU.mult)
+
+        out_v = out.rearrange("(p i) f -> p i f", i=RT)
+        nc.vector.tensor_scalar(out=z[:, 0, 0:512], in0=z[:, 0, 0:512], scalar1=factor[:, 0:1], scalar2=None, op0=ALU.mult)
+        nc.scalar.activation(out=z[:, 0, 512:1024], in_=z[:, 0, 512:1024], func=ACT.Copy, scale=factor[:, 0:1])
+        nc.sync.dma_start(out=out_v[:, 0, 0:512], in_=z[:, 0, 0:512])
+        nc.sync.dma_start(out=out_v[:, 0, 512:1024], in_=z[:, 0, 512:1024])
+        for i in range(1, RT):
+            nc.vector.tensor_scalar(out=z[:, i, :], in0=z[:, i, :], scalar1=factor[:, 0:1], scalar2=None, op0=ALU.mult)
+            nc.sync.dma_start(out=out_v[:, i, :], in_=z[:, i, :])

@@ -35,19 +35,17 @@ def tile_retentionmechanism_pb_kernel(tc, ao, w_qkv, out_w, tao, out):
 
         ident = keep.tile([P, P], F32)
         make_identity(nc, ident[:])
-        neg_half = keep.tile([P, 4], F32)
-        nc.gpsimd.memset(neg_half[:], -0.5)
         half = keep.tile([P, 1], F32)
         nc.gpsimd.memset(half[:], 0.5)
         ones = keep.tile([P, P], F32)
         nc.vector.memset(ones[:], 1.0)
         warm = keep.tile([P, 1], F32)
-        nc.vector.memset(warm[:], 0.0)
+        nc.vector.memset(warm[:], 1.0)
+        stats = keep.tile([P, 2, 32], F32)
+        nc.vector.memset(stats[:], 0.0)
 
-        tao_sb = keep.tile([P, 1], BF16)
-        nc.scalar.dma_start(out=tao_sb[:], in_=tao.partition_broadcast(P))
         warm_out = keep.tile([P, 1], F32)
-        nc.scalar.activation(out=warm_out[:], in_=warm[:], func=ACT.Silu)
+        nc.scalar.activation(out=warm_out[:], in_=warm[:], func=ACT.Sqrt)
 
         ao_sb = swap.tile([P, 2, 2, 2, E], BF16, tag="swap", align_bytes=64)
         ao_v = ao.rearrange("(c u p q) e -> c u p (q e)", c=2, u=2, q=2)
@@ -62,6 +60,8 @@ def tile_retentionmechanism_pb_kernel(tc, ao, w_qkv, out_w, tao, out):
         ow_v = out_w.rearrange("(h p) e -> p h e", p=P)
         nc.sync.dma_start(out=ow_sb[:, 0:4, :], in_=ow_v[:, 0:4, :])
         nc.sync.dma_start(out=ow_sb[:, 4:8, :], in_=ow_v[:, 4:8, :])
+        tao_sb = keep.tile([P, 1], BF16)
+        nc.sync.dma_start(out=tao_sb[:], in_=tao.partition_broadcast(P))
 
         early = big.tile([P, (RT + 8) * E], BF16, tag="big", align_bytes=64)
         w_grouped = early[:, 0 : RT * E].rearrange("p (i x) -> p i x", i=RT)
@@ -80,9 +80,8 @@ def tile_retentionmechanism_pb_kernel(tc, ao, w_qkv, out_w, tao, out):
         ss_v = keep.tile([P, 2, 2], F32)
         ss_s = keep.tile([P, 2, 2], F32)
         ms = keep.tile([P, 2, 2, 2], F32)
+        rms = keep.tile([P, 2, 2, 2], F32)
         rstd = keep.tile([P, 2, 4], F32)
-        s1 = keep.tile([P, 2 * RT], F32)
-        s2 = keep.tile([P, 2 * RT], F32)
         w_words = w_sb[:].bitcast(F32)
         o_words = ow_sb[:].bitcast(F32)
 
@@ -93,10 +92,15 @@ def tile_retentionmechanism_pb_kernel(tc, ao, w_qkv, out_w, tao, out):
             )
             nc.scalar.activation(out=junk_s[:], in_=ao_sb[:, c, u, 1, :], func=ACT.Square, accum_out=ss_s[:, c, u : u + 1])
 
-        def inverse_rms(c):
+        def mean_square(c):
             nc.vector.tensor_scalar(out=ms[:, c, :, 0], in0=ss_v[:, c, :], scalar1=1.0 / E, scalar2=EPS_RMS, op0=ALU.mult, op1=ALU.add)
             nc.vector.tensor_scalar(out=ms[:, c, :, 1], in0=ss_s[:, c, :], scalar1=1.0 / E, scalar2=EPS_RMS, op0=ALU.mult, op1=ALU.add)
-            nc.gpsimd.tensor_tensor(out=rstd[:, c, :], in0=ms[:, c].rearrange("p u q -> p (u q)"), in1=neg_half[:], op=ALU.pow)
+
+        def root_mean_square(c):
+            nc.scalar.activation(out=rms[:, c], in_=ms[:, c], func=ACT.Sqrt)
+
+        def inverse_rms(c):
+            nc.vector.reciprocal(out=rstd[:, c, :], in_=rms[:, c].rearrange("p u q -> p (u q)"))
 
         def scale_a(c, g):
             for j in range(4):
@@ -104,11 +108,13 @@ def tile_retentionmechanism_pb_kernel(tc, ao, w_qkv, out_w, tao, out):
                 nc.vector.tensor_scalar(out=part, in0=part, scalar1=rstd[:, c, j : j + 1], scalar2=None, op0=ALU.mult)
 
         def regroup_a(g, c):
-            src = ao_sb[:, c].rearrange("p u q e -> p (u q) e")[:, :, 512 * g : 512 * (g + 1)]
-            nc.vector.tensor_copy(
-                out=a_grouped[:, g, c].rearrange("p (v s m) j -> p v s m j", v=2, s=2),
-                in_=src.rearrange("p j (v m s) -> p v s m j", v=2, s=2),
-            )
+            rows = ao_sb[:, c].rearrange("p u q e -> p (u q) e")
+            for v in range(2):
+                first = 512 * g + 256 * v
+                nc.vector.tensor_copy(
+                    out=a_grouped[:, g, c, 256 * v : 256 * (v + 1), :].rearrange("p (s k m) j -> p k j m s", s=2, m=2),
+                    in_=rows[:, :, first : first + 256].rearrange("p j (k m s) -> p k j m s", m=2, s=2),
+                )
 
         def quantise_a(g):
             nc.vector.quantize_mx(
@@ -155,13 +161,19 @@ def tile_retentionmechanism_pb_kernel(tc, ao, w_qkv, out_w, tao, out):
                 in_=n_grouped[:, i].rearrange("p g r t -> p (g r t)"),
             )
 
-        for c in range(2):
-            for u in range(2):
-                sum_squares(c, u)
-            inverse_rms(c)
+        sum_squares(0, 0)
+        sum_squares(0, 1)
+        mean_square(0)
+        sum_squares(1, 0)
+        root_mean_square(0)
+        sum_squares(1, 1)
+        mean_square(1)
+        root_mean_square(1)
+        inverse_rms(0)
         for i in range(RT):
             transpose_w(i)
         scale_a(0, 0)
+        inverse_rms(1)
         regroup_a(0, 0)
         scale_a(1, 0)
         regroup_a(0, 1)
@@ -170,19 +182,11 @@ def tile_retentionmechanism_pb_kernel(tc, ao, w_qkv, out_w, tao, out):
         for i in range(1, LEAD):
             quantise_w(i)
 
-        tneg = keep.tile([P, 1], F32)
-        nc.vector.tensor_scalar(out=tneg[:], in0=tao_sb[:], scalar1=-1.0, scalar2=None, op0=ALU.mult)
-        tabs = keep.tile([P, 1], F32)
-        nc.vector.tensor_tensor(out=tabs[:], in0=tneg[:], in1=tao_sb[:], op=ALU.max)
-        tclip = keep.tile([P, 1], F32)
-        nc.vector.tensor_scalar(out=tclip[:], in0=tabs[:], scalar1=1e-08, scalar2=1.0, op0=ALU.max, op1=ALU.min)
-        gate = keep.tile([P, 1], F32)
-        nc.vector.tensor_scalar(out=gate[:], in0=tclip[:], scalar1=1.0 / 32.0, scalar2=None, op0=ALU.mult)
-
         scale_a(0, 1)
         regroup_a(1, 0)
         scale_a(1, 1)
         regroup_a(1, 1)
+        quantise_w(8)
         quantise_a(1)
 
         for i in range(LEAD):
@@ -210,7 +214,6 @@ def tile_retentionmechanism_pb_kernel(tc, ao, w_qkv, out_w, tao, out):
 
         for i in range(LEAD):
             multiply_one(i, 1)
-        quantise_w(8)
         quantise_o(0, 0)
         quantise_o(1, 0)
         quantise_n(0)
@@ -221,6 +224,15 @@ def tile_retentionmechanism_pb_kernel(tc, ao, w_qkv, out_w, tao, out):
             quantise_w(9 + k)
             quantise_n(2 + 2 * k)
             quantise_n(3 + 2 * k)
+
+        tneg = keep.tile([P, 1], F32)
+        nc.vector.tensor_scalar(out=tneg[:], in0=tao_sb[:], scalar1=-1.0, scalar2=None, op0=ALU.mult)
+        tabs = keep.tile([P, 1], F32)
+        nc.vector.tensor_tensor(out=tabs[:], in0=tneg[:], in1=tao_sb[:], op=ALU.max)
+        tclip = keep.tile([P, 1], F32)
+        nc.vector.tensor_scalar(out=tclip[:], in0=tabs[:], scalar1=1e-08, scalar2=1.0, op0=ALU.max, op1=ALU.min)
+        gate = keep.tile([P, 1], F32)
+        nc.vector.tensor_scalar(out=gate[:], in0=tclip[:], scalar1=1.0 / 32.0, scalar2=None, op0=ALU.mult)
 
         z = big.tile([P, RT, E], F32, tag="big", align_bytes=64)
 
@@ -240,13 +252,15 @@ def tile_retentionmechanism_pb_kernel(tc, ao, w_qkv, out_w, tao, out):
                 )
             nc.vector.scalar_tensor_tensor(
                 out=z[:, i, cols], in0=acc[:], scalar=1.0, in1=w_sb[:, i, cols],
-                op0=ALU.mult, op1=ALU.add, accum_out=s1[:, k : k + 1],
+                op0=ALU.mult, op1=ALU.add, accum_out=stats[:, 0, k : k + 1],
             )
 
-        def square_sum(k):
-            i, fh = k // 2, k % 2
+        def square_sum(i):
+            nc.scalar.activation(out=junk_s[:], in_=z[:, i, :], func=ACT.Square, accum_out=stats[:, 1, i : i + 1])
+
+        def square_sum_half(i, fh, k):
             nc.scalar.activation(
-                out=junk_s[:, 0:512], in_=z[:, i, 512 * fh : 512 * (fh + 1)], func=ACT.Square, accum_out=s2[:, k : k + 1]
+                out=junk_s[:, 0:512], in_=z[:, i, 512 * fh : 512 * (fh + 1)], func=ACT.Square, accum_out=stats[:, 1, k : k + 1]
             )
 
         squared = 0
@@ -256,20 +270,24 @@ def tile_retentionmechanism_pb_kernel(tc, ao, w_qkv, out_w, tao, out):
             for unit in range(4 * k, 4 * k + 4):
                 multiply_two(unit)
             quantise_n(LEAD + k)
-            while squared < 4 * k + 3:
+            while squared < 2 * k + 1:
                 square_sum(squared)
                 squared += 1
-        for unit in range(4 * (RT - LEAD), 2 * RT):
-            multiply_two(unit)
+        for i in range(2 * (RT - LEAD), RT):
+            multiply_two(2 * i)
+            multiply_two(2 * i + 1)
             square_sum(squared)
             squared += 1
-        while squared < 2 * RT:
+        while squared < RT - 1:
             square_sum(squared)
             squared += 1
+        square_sum_half(RT - 1, 0, RT - 1)
+        square_sum_half(RT - 1, 1, RT)
 
-        tot_ps = psum.tile([P, 2, 2 * RT], F32, tag="bank", name="tot_ps")
-        nc.tensor.matmul(out=tot_ps[:, 0, :], lhsT=ones[:], rhs=s1[:], start=True, stop=True)
-        nc.tensor.matmul(out=tot_ps[:, 1, :], lhsT=ones[:], rhs=s2[:], start=True, stop=True)
+        tot_ps = psum.tile([P, 2, 32], F32, tag="bank", name="tot_ps")
+        nc.tensor.matmul(
+            out=tot_ps[:].rearrange("p a k -> p (a k)"), lhsT=ones[:], rhs=stats[:].rearrange("p a k -> p (a k)"), start=True, stop=True
+        )
         tot = keep.tile([P, 2], F32)
         nc.vector.tensor_reduce(out=tot[:], in_=tot_ps[:], axis=AX.X, op=ALU.add)
         msq = keep.tile([P, 1], F32)
@@ -286,14 +304,16 @@ def tile_retentionmechanism_pb_kernel(tc, ao, w_qkv, out_w, tao, out):
         )
         inv = keep.tile([P, 1], F32)
         nc.vector.reciprocal(out=inv[:], in_=den[:])
-        factor = keep.tile([P, 1], F32)
-        nc.vector.tensor_tensor(out=factor[:], in0=inv[:], in1=gate[:], op=ALU.mult)
 
         out_v = out.rearrange("(p i) f -> p i f", i=RT)
-        nc.vector.tensor_scalar(out=z[:, 0, 0:512], in0=z[:, 0, 0:512], scalar1=factor[:, 0:1], scalar2=None, op0=ALU.mult)
-        nc.scalar.activation(out=z[:, 0, 512:1024], in_=z[:, 0, 512:1024], func=ACT.Copy, scale=factor[:, 0:1])
-        nc.sync.dma_start(out=out_v[:, 0, 0:512], in_=z[:, 0, 0:512])
-        nc.sync.dma_start(out=out_v[:, 0, 512:1024], in_=z[:, 0, 512:1024])
+
+        def scale_and_store(i, cols):
+            nc.vector.tensor_scalar(
+                out=z[:, i, cols], in0=z[:, i, cols], scalar1=inv[:, 0:1], scalar2=gate[:, 0:1], op0=ALU.mult, op1=ALU.mult
+            )
+            nc.sync.dma_start(out=out_v[:, i, cols], in_=z[:, i, cols])
+
+        scale_and_store(0, slice(0, 512))
+        scale_and_store(0, slice(512, 1024))
         for i in range(1, RT):
-            nc.vector.tensor_scalar(out=z[:, i, :], in0=z[:, i, :], scalar1=factor[:, 0:1], scalar2=None, op0=ALU.mult)
-            nc.sync.dma_start(out=out_v[:, i, :], in_=z[:, i, :])
+            scale_and_store(i, slice(0, 1024))

@@ -161,10 +161,16 @@ def tile_retentionmechanism_pb_kernel(tc, ao, w_qkv, out_w, tao, out):
                 in_=n_grouped[:, i].rearrange("p g r t -> p (g r t)"),
             )
 
+        def keep_clock_up(operand):
+            idle = psum.tile([P, 512], F32, tag="bank", name="idle")
+            nc.tensor.matmul(out=idle[:], lhsT=operand[:, 0:P], rhs=operand[:, 0:512], start=True, stop=True)
+
         sum_squares(0, 0)
         sum_squares(0, 1)
         mean_square(0)
         sum_squares(1, 0)
+        for k in range(4):
+            keep_clock_up(ao_sb[:, 1, 0, 0, :])
         root_mean_square(0)
         sum_squares(1, 1)
         mean_square(1)
@@ -172,6 +178,8 @@ def tile_retentionmechanism_pb_kernel(tc, ao, w_qkv, out_w, tao, out):
         inverse_rms(0)
         for i in range(RT):
             transpose_w(i)
+            if i % 2 == 1:
+                keep_clock_up(w_sb[:, i, :])
         scale_a(0, 0)
         inverse_rms(1)
         regroup_a(0, 0)
@@ -237,9 +245,11 @@ def tile_retentionmechanism_pb_kernel(tc, ao, w_qkv, out_w, tao, out):
         z = big.tile([P, RT, E], F32, tag="big", align_bytes=64)
 
         def multiply_two(k):
-            i, fh = k // 2, k % 2
-            cols = slice(512 * fh, 512 * (fh + 1))
-            acc = psum.tile([P, 512], F32, tag="bank", name="acc2")
+            multiply_two_part(k // 2, 512 * (k % 2), 512, k)
+
+        def multiply_two_part(i, first, width, k):
+            cols = slice(first, first + width)
+            acc = psum.tile([P, width], F32, tag="bank", name="acc2")
             for g in range(2):
                 nc.tensor.matmul_mx(
                     out=acc[:],
@@ -258,9 +268,9 @@ def tile_retentionmechanism_pb_kernel(tc, ao, w_qkv, out_w, tao, out):
         def square_sum(i):
             nc.scalar.activation(out=junk_s[:], in_=z[:, i, :], func=ACT.Square, accum_out=stats[:, 1, i : i + 1])
 
-        def square_sum_half(i, fh, k):
+        def square_sum_part(i, first, width, k):
             nc.scalar.activation(
-                out=junk_s[:, 0:512], in_=z[:, i, 512 * fh : 512 * (fh + 1)], func=ACT.Square, accum_out=stats[:, 1, k : k + 1]
+                out=junk_s[:, 0:width], in_=z[:, i, first : first + width], func=ACT.Square, accum_out=stats[:, 1, k : k + 1]
             )
 
         squared = 0
@@ -273,16 +283,18 @@ def tile_retentionmechanism_pb_kernel(tc, ao, w_qkv, out_w, tao, out):
             while squared < 2 * k + 1:
                 square_sum(squared)
                 squared += 1
-        for i in range(2 * (RT - LEAD), RT):
+        for i in range(2 * (RT - LEAD), RT - 1):
             multiply_two(2 * i)
             multiply_two(2 * i + 1)
             square_sum(squared)
             squared += 1
-        while squared < RT - 1:
-            square_sum(squared)
-            squared += 1
-        square_sum_half(RT - 1, 0, RT - 1)
-        square_sum_half(RT - 1, 1, RT)
+        multiply_two(2 * RT - 2)
+        square_sum(squared)
+        multiply_two_part(RT - 1, 512, 256, 2 * RT - 1)
+        square_sum_part(RT - 1, 0, 512, RT - 1)
+        multiply_two_part(RT - 1, 768, 256, 2 * RT)
+        square_sum_part(RT - 1, 512, 256, RT)
+        square_sum_part(RT - 1, 768, 256, RT + 1)
 
         tot_ps = psum.tile([P, 2, 32], F32, tag="bank", name="tot_ps")
         nc.tensor.matmul(
@@ -307,13 +319,17 @@ def tile_retentionmechanism_pb_kernel(tc, ao, w_qkv, out_w, tao, out):
 
         out_v = out.rearrange("(p i) f -> p i f", i=RT)
 
-        def scale_and_store(i, cols):
+        def scale(i, cols):
             nc.vector.tensor_scalar(
                 out=z[:, i, cols], in0=z[:, i, cols], scalar1=inv[:, 0:1], scalar2=gate[:, 0:1], op0=ALU.mult, op1=ALU.mult
             )
-            nc.sync.dma_start(out=out_v[:, i, cols], in_=z[:, i, cols])
 
-        scale_and_store(0, slice(0, 512))
-        scale_and_store(0, slice(512, 1024))
-        for i in range(1, RT):
-            scale_and_store(i, slice(0, 1024))
+        for cols in (slice(0, 512), slice(512, 1024)):
+            scale(0, cols)
+            nc.sync.dma_start(out=out_v[:, 0, cols], in_=z[:, 0, cols])
+        first = 1
+        for count in (1, 2, 4, 4):
+            for i in range(first, first + count):
+                scale(i, slice(0, 1024))
+            nc.sync.dma_start(out=out_v[:, first : first + count, :], in_=z[:, first : first + count, :])
+            first += count

@@ -161,16 +161,10 @@ def tile_retentionmechanism_pb_kernel(tc, ao, w_qkv, out_w, tao, out):
                 in_=n_grouped[:, i].rearrange("p g r t -> p (g r t)"),
             )
 
-        def keep_clock_up(operand):
-            idle = psum.tile([P, 512], F32, tag="bank", name="idle")
-            nc.tensor.matmul(out=idle[:], lhsT=operand[:, 0:P], rhs=operand[:, 0:512], start=True, stop=True)
-
         sum_squares(0, 0)
         sum_squares(0, 1)
         mean_square(0)
         sum_squares(1, 0)
-        for k in range(4):
-            keep_clock_up(ao_sb[:, 1, 0, 0, :])
         root_mean_square(0)
         sum_squares(1, 1)
         mean_square(1)
@@ -178,8 +172,6 @@ def tile_retentionmechanism_pb_kernel(tc, ao, w_qkv, out_w, tao, out):
         inverse_rms(0)
         for i in range(RT):
             transpose_w(i)
-            if i % 2 == 1:
-                keep_clock_up(w_sb[:, i, :])
         scale_a(0, 0)
         inverse_rms(1)
         regroup_a(0, 0)
@@ -233,14 +225,14 @@ def tile_retentionmechanism_pb_kernel(tc, ao, w_qkv, out_w, tao, out):
             quantise_n(2 + 2 * k)
             quantise_n(3 + 2 * k)
 
-        tneg = keep.tile([P, 1], F32)
-        nc.vector.tensor_scalar(out=tneg[:], in0=tao_sb[:], scalar1=-1.0, scalar2=None, op0=ALU.mult)
+        tsq = keep.tile([P, 1], F32)
+        nc.gpsimd.tensor_tensor(out=tsq[:], in0=tao_sb[:], in1=tao_sb[:], op=ALU.mult)
         tabs = keep.tile([P, 1], F32)
-        nc.vector.tensor_tensor(out=tabs[:], in0=tneg[:], in1=tao_sb[:], op=ALU.max)
+        nc.gpsimd.tensor_tensor(out=tabs[:], in0=tsq[:], in1=half[:], op=ALU.pow)
         tclip = keep.tile([P, 1], F32)
-        nc.vector.tensor_scalar(out=tclip[:], in0=tabs[:], scalar1=1e-08, scalar2=1.0, op0=ALU.max, op1=ALU.min)
+        nc.gpsimd.tensor_scalar(out=tclip[:], in0=tabs[:], scalar1=1e-08, scalar2=1.0, op0=ALU.max, op1=ALU.min)
         gate = keep.tile([P, 1], F32)
-        nc.vector.tensor_scalar(out=gate[:], in0=tclip[:], scalar1=1.0 / 32.0, scalar2=None, op0=ALU.mult)
+        nc.gpsimd.tensor_scalar(out=gate[:], in0=tclip[:], scalar1=1.0 / 32.0, scalar2=0.0, op0=ALU.mult, op1=ALU.add)
 
         z = big.tile([P, RT, E], F32, tag="big", align_bytes=64)
 
@@ -319,17 +311,13 @@ def tile_retentionmechanism_pb_kernel(tc, ao, w_qkv, out_w, tao, out):
 
         out_v = out.rearrange("(p i) f -> p i f", i=RT)
 
-        def scale(i, cols):
+        def scale_and_store(i, cols):
             nc.vector.tensor_scalar(
                 out=z[:, i, cols], in0=z[:, i, cols], scalar1=inv[:, 0:1], scalar2=gate[:, 0:1], op0=ALU.mult, op1=ALU.mult
             )
+            nc.sync.dma_start(out=out_v[:, i, cols], in_=z[:, i, cols])
 
-        for cols in (slice(0, 512), slice(512, 1024)):
-            scale(0, cols)
-            nc.sync.dma_start(out=out_v[:, 0, cols], in_=z[:, 0, cols])
-        first = 1
-        for count in (1, 2, 4, 4):
-            for i in range(first, first + count):
-                scale(i, slice(0, 1024))
-            nc.sync.dma_start(out=out_v[:, first : first + count, :], in_=z[:, first : first + count, :])
-            first += count
+        scale_and_store(0, slice(0, 512))
+        scale_and_store(0, slice(512, 1024))
+        for i in range(1, RT):
+            scale_and_store(i, slice(0, 1024))

@@ -45,7 +45,7 @@ def tile_retentionmechanism_pb_kernel(tc, ao, w_qkv, out_w, tao, out):
         nc.vector.memset(stats[:], 0.0)
 
         warm_out = keep.tile([P, 1], F32)
-        nc.scalar.activation(out=warm_out[:], in_=warm[:], func=ACT.Sqrt)
+        nc.scalar.activation(out=warm_out[:], in_=warm[:], func=ACT.Abs_reciprocal_sqrt)
 
         ao_sb = swap.tile([P, 2, 2, 2, E], BF16, tag="swap", align_bytes=64)
         ao_v = ao.rearrange("(c u p q) e -> c u p (q e)", c=2, u=2, q=2)
@@ -80,7 +80,6 @@ def tile_retentionmechanism_pb_kernel(tc, ao, w_qkv, out_w, tao, out):
         ss_v = keep.tile([P, 2, 2], F32)
         ss_s = keep.tile([P, 2, 2], F32)
         ms = keep.tile([P, 2, 2, 2], F32)
-        rms = keep.tile([P, 2, 2, 2], F32)
         rstd = keep.tile([P, 2, 4], F32)
         w_words = w_sb[:].bitcast(F32)
         o_words = ow_sb[:].bitcast(F32)
@@ -96,11 +95,8 @@ def tile_retentionmechanism_pb_kernel(tc, ao, w_qkv, out_w, tao, out):
             nc.vector.tensor_scalar(out=ms[:, c, :, 0], in0=ss_v[:, c, :], scalar1=1.0 / E, scalar2=EPS_RMS, op0=ALU.mult, op1=ALU.add)
             nc.vector.tensor_scalar(out=ms[:, c, :, 1], in0=ss_s[:, c, :], scalar1=1.0 / E, scalar2=EPS_RMS, op0=ALU.mult, op1=ALU.add)
 
-        def root_mean_square(c):
-            nc.scalar.activation(out=rms[:, c], in_=ms[:, c], func=ACT.Sqrt)
-
         def inverse_rms(c):
-            nc.vector.reciprocal(out=rstd[:, c, :], in_=rms[:, c].rearrange("p u q -> p (u q)"))
+            nc.scalar.activation(out=rstd[:, c, :], in_=ms[:, c].rearrange("p u q -> p (u q)"), func=ACT.Abs_reciprocal_sqrt)
 
         def scale_a(c, g):
             for j in range(4):
@@ -165,15 +161,13 @@ def tile_retentionmechanism_pb_kernel(tc, ao, w_qkv, out_w, tao, out):
         sum_squares(0, 1)
         mean_square(0)
         sum_squares(1, 0)
-        root_mean_square(0)
+        inverse_rms(0)
         sum_squares(1, 1)
         mean_square(1)
-        root_mean_square(1)
-        inverse_rms(0)
+        inverse_rms(1)
         for i in range(RT):
             transpose_w(i)
         scale_a(0, 0)
-        inverse_rms(1)
         regroup_a(0, 0)
         scale_a(1, 0)
         regroup_a(0, 1)

@@ -51,7 +51,11 @@ def tile_retentionmechanism_pb_kernel(tc, ao, w_qkv, out_w, tao, out):
         ao_v = ao.rearrange("(c u p q) e -> c u p (q e)", c=2, u=2, q=2)
         for c in range(2):
             for u in range(2):
-                nc.sync.dma_start(out=ao_sb[:, c, u].rearrange("p q e -> p (q e)"), in_=ao_v[c, u])
+                if c == 0 and u == 0:
+                    for q in range(2):
+                        nc.sync.dma_start(out=ao_sb[:, c, u, q], in_=ao_v[c, u, :, q * E : (q + 1) * E])
+                else:
+                    nc.sync.dma_start(out=ao_sb[:, c, u].rearrange("p q e -> p (q e)"), in_=ao_v[c, u])
         w_sb = keep.tile([P, RT, E], BF16)
         w_v = w_qkv.rearrange("(p i) d -> p i d", i=RT)
         for i in range(0, RT, 2):
@@ -77,9 +81,7 @@ def tile_retentionmechanism_pb_kernel(tc, ao, w_qkv, out_w, tao, out):
         n_scales = keep.tile([P, RT, 2, P], U8, align_bytes=64)
         junk_v = keep.tile([P, E], BF16)
         junk_s = keep.tile([P, E], BF16)
-        ss_v = keep.tile([P, 2, 2], F32)
-        ss_s = keep.tile([P, 2, 2], F32)
-        ms = keep.tile([P, 2, 2, 2], F32)
+        ss = keep.tile([P, 2, 4], F32)
         rstd = keep.tile([P, 2, 4], F32)
         w_words = w_sb[:].bitcast(F32)
         o_words = ow_sb[:].bitcast(F32)
@@ -87,16 +89,16 @@ def tile_retentionmechanism_pb_kernel(tc, ao, w_qkv, out_w, tao, out):
         def sum_squares(c, u):
             nc.vector.scalar_tensor_tensor(
                 out=junk_v[:], in0=ao_sb[:, c, u, 0, :], scalar=1.0, in1=ao_sb[:, c, u, 0, :],
-                op0=ALU.mult, op1=ALU.mult, accum_out=ss_v[:, c, u : u + 1],
+                op0=ALU.mult, op1=ALU.mult, accum_out=ss[:, c, 2 * u : 2 * u + 1],
             )
-            nc.scalar.activation(out=junk_s[:], in_=ao_sb[:, c, u, 1, :], func=ACT.Square, accum_out=ss_s[:, c, u : u + 1])
-
-        def mean_square(c):
-            nc.vector.tensor_scalar(out=ms[:, c, :, 0], in0=ss_v[:, c, :], scalar1=1.0 / E, scalar2=EPS_RMS, op0=ALU.mult, op1=ALU.add)
-            nc.vector.tensor_scalar(out=ms[:, c, :, 1], in0=ss_s[:, c, :], scalar1=1.0 / E, scalar2=EPS_RMS, op0=ALU.mult, op1=ALU.add)
+            nc.scalar.activation(
+                out=junk_s[:], in_=ao_sb[:, c, u, 1, :], func=ACT.Square, accum_out=ss[:, c, 2 * u + 1 : 2 * u + 2]
+            )
 
         def inverse_rms(c):
-            nc.scalar.activation(out=rstd[:, c, :], in_=ms[:, c].rearrange("p u q -> p (u q)"), func=ACT.Abs_reciprocal_sqrt)
+            nc.scalar.activation(
+                out=rstd[:, c, :], in_=ss[:, c, :], func=ACT.Abs_reciprocal_sqrt, scale=1.0 / E, bias=EPS_RMS
+            )
 
         def scale_a(c, g):
             for j in range(4):
@@ -159,11 +161,9 @@ def tile_retentionmechanism_pb_kernel(tc, ao, w_qkv, out_w, tao, out):
 
         sum_squares(0, 0)
         sum_squares(0, 1)
-        mean_square(0)
         sum_squares(1, 0)
         inverse_rms(0)
         sum_squares(1, 1)
-        mean_square(1)
         inverse_rms(1)
         for i in range(RT):
             transpose_w(i)
@@ -219,14 +219,10 @@ def tile_retentionmechanism_pb_kernel(tc, ao, w_qkv, out_w, tao, out):
             quantise_n(2 + 2 * k)
             quantise_n(3 + 2 * k)
 
-        tsq = keep.tile([P, 1], F32)
-        nc.gpsimd.tensor_tensor(out=tsq[:], in0=tao_sb[:], in1=tao_sb[:], op=ALU.mult)
         tabs = keep.tile([P, 1], F32)
-        nc.gpsimd.tensor_tensor(out=tabs[:], in0=tsq[:], in1=half[:], op=ALU.pow)
-        tclip = keep.tile([P, 1], F32)
-        nc.gpsimd.tensor_scalar(out=tclip[:], in0=tabs[:], scalar1=1e-08, scalar2=1.0, op0=ALU.max, op1=ALU.min)
+        nc.scalar.activation(out=tabs[:], in_=tao_sb[:], func=ACT.Abs)
         gate = keep.tile([P, 1], F32)
-        nc.gpsimd.tensor_scalar(out=gate[:], in0=tclip[:], scalar1=1.0 / 32.0, scalar2=0.0, op0=ALU.mult, op1=ALU.add)
+        nc.vector.tensor_scalar(out=gate[:], in0=tabs[:], scalar1=1e-08, scalar2=1.0, op0=ALU.max, op1=ALU.min)
 
         z = big.tile([P, RT, E], F32, tag="big", align_bytes=64)
 
@@ -298,7 +294,7 @@ def tile_retentionmechanism_pb_kernel(tc, ao, w_qkv, out_w, tao, out):
         nc.gpsimd.tensor_tensor(out=root[:], in0=dev[:], in1=half[:], op=ALU.pow)
         den = keep.tile([P, 1], F32)
         nc.vector.tensor_scalar(
-            out=den[:], in0=root[:], scalar1=(COUNT - 1.0) ** -0.5, scalar2=1e-08, op0=ALU.mult, op1=ALU.add
+            out=den[:], in0=root[:], scalar1=32.0 * (COUNT - 1.0) ** -0.5, scalar2=32.0 * 1e-08, op0=ALU.mult, op1=ALU.add
         )
         inv = keep.tile([P, 1], F32)
         nc.vector.reciprocal(out=inv[:], in_=den[:])

@@ -35,8 +35,6 @@ def tile_retentionmechanism_pb_kernel(tc, ao, w_qkv, out_w, tao, out):
 
         ident = keep.tile([P, P], F32)
         make_identity(nc, ident[:])
-        half = keep.tile([P, 1], F32)
-        nc.gpsimd.memset(half[:], 0.5)
         ones = keep.tile([P, P], F32)
         nc.vector.memset(ones[:], 1.0)
         warm = keep.tile([P, 1], F32)
@@ -250,11 +248,6 @@ def tile_retentionmechanism_pb_kernel(tc, ao, w_qkv, out_w, tao, out):
         def square_sum(i):
             nc.scalar.activation(out=junk_s[:], in_=z[:, i, :], func=ACT.Square, accum_out=stats[:, 1, i : i + 1])
 
-        def square_sum_part(i, first, width, k):
-            nc.scalar.activation(
-                out=junk_s[:, 0:width], in_=z[:, i, first : first + width], func=ACT.Square, accum_out=stats[:, 1, k : k + 1]
-            )
-
         squared = 0
         for k in range(RT - LEAD):
             multiply_one(LEAD + k, 0)
@@ -270,32 +263,39 @@ def tile_retentionmechanism_pb_kernel(tc, ao, w_qkv, out_w, tao, out):
             multiply_two(2 * i + 1)
             square_sum(squared)
             squared += 1
-        multiply_two(2 * RT - 2)
+        last = RT - 1
+        multiply_two(2 * last)
         square_sum(squared)
-        multiply_two_part(RT - 1, 512, 256, 2 * RT - 1)
-        square_sum_part(RT - 1, 0, 512, RT - 1)
-        multiply_two_part(RT - 1, 768, 256, 2 * RT)
-        square_sum_part(RT - 1, 512, 256, RT)
-        square_sum_part(RT - 1, 768, 256, RT + 1)
+        nc.scalar.activation(out=warm_out[:], in_=warm[:], func=ACT.Sqrt)
+        multiply_two_part(last, 512, 256, 2 * last + 1)
+        multiply_two_part(last, 768, 256, 2 * last + 2)
 
-        tot_ps = psum.tile([P, 2, 32], F32, tag="bank", name="tot_ps")
-        nc.tensor.matmul(
-            out=tot_ps[:].rearrange("p a k -> p (a k)"), lhsT=ones[:], rhs=stats[:].rearrange("p a k -> p (a k)"), start=True, stop=True
-        )
-        tot = keep.tile([P, 2], F32)
-        nc.vector.tensor_reduce(out=tot[:], in_=tot_ps[:], axis=AX.X, op=ALU.add)
-        msq = keep.tile([P, 1], F32)
-        nc.vector.scalar_tensor_tensor(
-            out=msq[:], in0=tot[:, 0:1], scalar=-1.0 / COUNT, in1=tot[:, 0:1], op0=ALU.mult, op1=ALU.mult
-        )
-        dev = keep.tile([P, 1], F32)
-        nc.vector.tensor_scalar(out=dev[:], in0=msq[:], scalar1=tot[:, 1:2], scalar2=0.0, op0=ALU.add, op1=ALU.max)
-        root = keep.tile([P, 1], F32)
-        nc.gpsimd.tensor_tensor(out=root[:], in0=dev[:], in1=half[:], op=ALU.pow)
-        den = keep.tile([P, 1], F32)
+        def square_sum_on_vector(first, width, out):
+            part = z[:, last, first : first + width]
+            nc.vector.scalar_tensor_tensor(
+                out=junk_v[:, 0:width], in0=part, scalar=1.0, in1=part, op0=ALU.mult, op1=ALU.mult, accum_out=out
+            )
+
+        sums = keep.tile([P, 2], F32)
+        last_square = keep.tile([P, 1], F32)
+        square_sum_on_vector(0, 512, stats[:, 1, last : last + 1])
+        nc.vector.tensor_reduce(out=sums[:, 0:1], in_=stats[:, 0, :], axis=AX.X, op=ALU.add)
+        nc.vector.tensor_reduce(out=sums[:, 1:2], in_=stats[:, 1, :], axis=AX.X, op=ALU.add)
+        square_sum_on_vector(512, 512, last_square[:])
+
+        total = psum.tile([P, 1], F32, tag="bank", name="total")
+        nc.tensor.matmul(out=total[:], lhsT=ones[:], rhs=sums[:, 0:1], start=True, stop=True)
+        mean_part = keep.tile([P, 1], F32)
         nc.vector.tensor_scalar(
-            out=den[:], in0=root[:], scalar1=32.0 * (COUNT - 1.0) ** -0.5, scalar2=32.0 * 1e-08, op0=ALU.mult, op1=ALU.add
+            out=mean_part[:], in0=total[:], scalar1=-1024.0 / COUNT / (COUNT - 1.0), scalar2=total[:, 0:1], op0=ALU.mult, op1=ALU.mult
         )
+        total_sq = psum.tile([P, 1], F32, tag="bank", name="total_sq")
+        nc.tensor.matmul(out=total_sq[:], lhsT=ones[:], rhs=sums[:, 1:2], start=True, stop=False)
+        nc.tensor.matmul(out=total_sq[:], lhsT=ones[:], rhs=last_square[:], start=False, stop=True)
+        root = keep.tile([P, 1], F32)
+        nc.scalar.activation(out=root[:], in_=total_sq[:], func=ACT.Sqrt, scale=1024.0 / (COUNT - 1.0), bias=mean_part[:])
+        den = keep.tile([P, 1], F32)
+        nc.vector.tensor_scalar(out=den[:], in0=root[:], scalar1=32.0 * 1e-08, scalar2=None, op0=ALU.add)
         inv = keep.tile([P, 1], F32)
         nc.vector.reciprocal(out=inv[:], in_=den[:])
 

@@ -166,8 +166,8 @@ def tile_retentionmechanism_pb_kernel(tc, ao, w_qkv, out_w, tao, out):
         for i in range(RT):
             transpose_w(i)
         scale_a(0, 0)
-        regroup_a(0, 0)
         scale_a(1, 0)
+        regroup_a(0, 0)
         regroup_a(0, 1)
         quantise_w(0)
         quantise_a(0)
@@ -175,8 +175,8 @@ def tile_retentionmechanism_pb_kernel(tc, ao, w_qkv, out_w, tao, out):
             quantise_w(i)
 
         scale_a(0, 1)
-        regroup_a(1, 0)
         scale_a(1, 1)
+        regroup_a(1, 0)
         regroup_a(1, 1)
         quantise_w(8)
         quantise_a(1)
@@ -219,8 +219,6 @@ def tile_retentionmechanism_pb_kernel(tc, ao, w_qkv, out_w, tao, out):
 
         tabs = keep.tile([P, 1], F32)
         nc.scalar.activation(out=tabs[:], in_=tao_sb[:], func=ACT.Abs)
-        gate = keep.tile([P, 1], F32)
-        nc.vector.tensor_scalar(out=gate[:], in0=tabs[:], scalar1=1e-08, scalar2=1.0, op0=ALU.max, op1=ALU.min)
 
         z = big.tile([P, RT, E], F32, tag="big", align_bytes=64)
 
@@ -249,20 +247,17 @@ def tile_retentionmechanism_pb_kernel(tc, ao, w_qkv, out_w, tao, out):
             nc.scalar.activation(out=junk_s[:], in_=z[:, i, :], func=ACT.Square, accum_out=stats[:, 1, i : i + 1])
 
         squared = 0
-        for k in range(RT - LEAD):
-            multiply_one(LEAD + k, 0)
-            multiply_one(LEAD + k, 1)
-            for unit in range(4 * k, 4 * k + 4):
-                multiply_two(unit)
-            quantise_n(LEAD + k)
-            while squared < 2 * k + 1:
-                square_sum(squared)
-                squared += 1
-        for i in range(2 * (RT - LEAD), RT - 1):
+        for i in range(RT - 1):
+            if i % 3 == 0:
+                multiply_one(LEAD + i // 3, 0)
+                multiply_one(LEAD + i // 3, 1)
             multiply_two(2 * i)
             multiply_two(2 * i + 1)
-            square_sum(squared)
-            squared += 1
+            if i % 3 == 0:
+                quantise_n(LEAD + i // 3)
+            if i > 0:
+                square_sum(squared)
+                squared += 1
         last = RT - 1
         multiply_two(2 * last)
         square_sum(squared)
@@ -285,6 +280,8 @@ def tile_retentionmechanism_pb_kernel(tc, ao, w_qkv, out_w, tao, out):
 
         total = psum.tile([P, 1], F32, tag="bank", name="total")
         nc.tensor.matmul(out=total[:], lhsT=ones[:], rhs=sums[:, 0:1], start=True, stop=True)
+        gate = keep.tile([P, 1], F32)
+        nc.vector.tensor_scalar(out=gate[:], in0=tabs[:], scalar1=1e-08, scalar2=1.0, op0=ALU.max, op1=ALU.min)
         mean_part = keep.tile([P, 1], F32)
         nc.vector.tensor_scalar(
             out=mean_part[:], in0=total[:], scalar1=-1024.0 / COUNT / (COUNT - 1.0), scalar2=total[:, 0:1], op0=ALU.mult, op1=ALU.mult
@@ -301,13 +298,13 @@ def tile_retentionmechanism_pb_kernel(tc, ao, w_qkv, out_w, tao, out):
 
         out_v = out.rearrange("(p i) f -> p i f", i=RT)
 
-        def scale_and_store(i, cols):
+        def scale_and_store(i, cols, queue):
             nc.vector.tensor_scalar(
                 out=z[:, i, cols], in0=z[:, i, cols], scalar1=inv[:, 0:1], scalar2=gate[:, 0:1], op0=ALU.mult, op1=ALU.mult
             )
-            nc.sync.dma_start(out=out_v[:, i, cols], in_=z[:, i, cols])
+            queue.dma_start(out=out_v[:, i, cols], in_=z[:, i, cols])
 
-        scale_and_store(0, slice(0, 512))
-        scale_and_store(0, slice(512, 1024))
+        scale_and_store(0, slice(0, 512), nc.sync)
+        scale_and_store(0, slice(512, 1024), nc.scalar)
         for i in range(1, RT):
-            scale_and_store(i, slice(0, 1024))
+            scale_and_store(i, slice(0, 1024), nc.sync if i % 2 == 1 else nc.scalar)

@@ -163,7 +163,8 @@ def tile_retentionmechanism_pb_kernel(tc, ao, w_qkv, out_w, tao, out):
         inverse_rms(0)
         sum_squares(1, 1)
         inverse_rms(1)
-        for i in range(RT):
+        nc.scalar.activation(out=warm_out[:], in_=warm[:], func=ACT.Silu)
+        for i in range(LEAD + 2):
             transpose_w(i)
         scale_a(0, 0)
         scale_a(1, 0)
@@ -183,6 +184,8 @@ def tile_retentionmechanism_pb_kernel(tc, ao, w_qkv, out_w, tao, out):
 
         for i in range(LEAD):
             multiply_one(i, 0)
+        for i in range(LEAD + 2, RT):
+            transpose_w(i)
 
         o_grouped = swap.tile([P, 2, 4 * E], BF16, tag="swap", align_bytes=64)
         o_grouped_words = o_grouped[:].bitcast(F32).rearrange("p g (f v) -> p g f v", v=2)
@@ -264,6 +267,10 @@ def tile_retentionmechanism_pb_kernel(tc, ao, w_qkv, out_w, tao, out):
         nc.scalar.activation(out=warm_out[:], in_=warm[:], func=ACT.Sqrt)
         multiply_two_part(last, 512, 256, 2 * last + 1)
         multiply_two_part(last, 768, 256, 2 * last + 2)
+
+        idle = psum.tile([P, 512], F32, tag="bank", name="idle")
+        for k in range(8):
+            nc.tensor.matmul(out=idle[:], lhsT=w_sb[:, 0, 0:P], rhs=w_sb[:, 0, 0:512], start=True, stop=True)
 
         def square_sum_on_vector(first, width, out):
             part = z[:, last, first : first + width]

@@ -45,7 +45,7 @@ def tile_retentionmechanism_pb_kernel(tc, ao, w_qkv, out_w, tao, out):
         warm_out = keep.tile([P, 1], F32)
         nc.scalar.activation(out=warm_out[:], in_=warm[:], func=ACT.Abs_reciprocal_sqrt)
 
-        ao_sb = swap.tile([P, 2, 2, 2, E], BF16, tag="swap", align_bytes=64)
+        ao_sb = swap.tile([P, 2, 2, 2, E], BF16, tag="swap", align_bytes=256)
         ao_v = ao.rearrange("(c u p q) e -> c u p (q e)", c=2, u=2, q=2)
         for c in range(2):
             for u in range(2):
@@ -65,18 +65,18 @@ def tile_retentionmechanism_pb_kernel(tc, ao, w_qkv, out_w, tao, out):
         tao_sb = keep.tile([P, 1], BF16)
         nc.sync.dma_start(out=tao_sb[:], in_=tao.partition_broadcast(P))
 
-        early = big.tile([P, (RT + 8) * E], BF16, tag="big", align_bytes=64)
+        early = big.tile([P, (RT + 8) * E], BF16, tag="big", align_bytes=256)
         w_grouped = early[:, 0 : RT * E].rearrange("p (i x) -> p i x", i=RT)
         a_grouped = early[:, RT * E : (RT + 8) * E].rearrange("p (g c w j) -> p g c w j", g=2, c=2, j=4)
-        a_codes = keep.tile([P, 2, 2, 512], U32, align_bytes=64)
-        a_scales = keep.tile([P, 2, 2, 512], U8, align_bytes=64)
-        w_codes = keep.tile([P, RT, 2, P], U32, align_bytes=64)
-        w_scales = keep.tile([P, RT, 2, P], U8, align_bytes=64)
-        o_codes = keep.tile([P, 2, E], U32, align_bytes=64)
-        o_scales = keep.tile([P, 2, E], U8, align_bytes=64)
-        n_grouped = keep.tile([P, RT, 2, P, 4], BF16, align_bytes=64)
-        n_codes = keep.tile([P, RT, 2, P], U32, align_bytes=64)
-        n_scales = keep.tile([P, RT, 2, P], U8, align_bytes=64)
+        a_codes = keep.tile([P, 2, 2, 512], U32, align_bytes=256)
+        a_scales = keep.tile([P, 2, 2, 512], U8, align_bytes=256)
+        w_codes = keep.tile([P, RT, 2, P], U32, align_bytes=256)
+        w_scales = keep.tile([P, RT, 2, P], U8, align_bytes=256)
+        o_codes = keep.tile([P, 2, E], U32, align_bytes=256)
+        o_scales = keep.tile([P, 2, E], U8, align_bytes=256)
+        n_grouped = keep.tile([P, RT, 2, P, 4], BF16, align_bytes=256)
+        n_codes = keep.tile([P, RT, 2, P], U32, align_bytes=256)
+        n_scales = keep.tile([P, RT, 2, P], U8, align_bytes=256)
         junk_v = keep.tile([P, E], BF16)
         junk_s = keep.tile([P, E], BF16)
         ss = keep.tile([P, 2, 4], F32)
@@ -187,7 +187,7 @@ def tile_retentionmechanism_pb_kernel(tc, ao, w_qkv, out_w, tao, out):
         for i in range(LEAD + 2, RT):
             transpose_w(i)
 
-        o_grouped = swap.tile([P, 2, 4 * E], BF16, tag="swap", align_bytes=64)
+        o_grouped = swap.tile([P, 2, 4 * E], BF16, tag="swap", align_bytes=256)
         o_grouped_words = o_grouped[:].bitcast(F32).rearrange("p g (f v) -> p g f v", v=2)
         for h in range(FT):
             xt = psum.tile([P, 4, P], F32, tag="bank", name="xt")
@@ -223,7 +223,7 @@ def tile_retentionmechanism_pb_kernel(tc, ao, w_qkv, out_w, tao, out):
         tabs = keep.tile([P, 1], F32)
         nc.scalar.activation(out=tabs[:], in_=tao_sb[:], func=ACT.Abs)
 
-        z = big.tile([P, RT, E], F32, tag="big", align_bytes=64)
+        z = big.tile([P, RT, E], F32, tag="big", align_bytes=256)
 
         def multiply_two(k):
             multiply_two_part(k // 2, 512 * (k % 2), 512, k)
@@ -311,7 +311,7 @@ def tile_retentionmechanism_pb_kernel(tc, ao, w_qkv, out_w, tao, out):
             )
             queue.dma_start(out=out_v[:, i, cols], in_=z[:, i, cols])
 
-        scale_and_store(0, slice(0, 512), nc.sync)
-        scale_and_store(0, slice(512, 1024), nc.scalar)
+        for k in range(4):
+            scale_and_store(0, slice(256 * k, 256 * (k + 1)), nc.sync if k % 2 == 0 else nc.scalar)
         for i in range(1, RT):
             scale_and_store(i, slice(0, 1024), nc.sync if i % 2 == 1 else nc.scalar)

@@ -207,7 +207,7 @@ def tile_retentionmechanism_pb_kernel(tc, ao, w_qkv, out_w, tao, out):
                 in_=o_grouped[:, g, 2048 * fh : 2048 * (fh + 1)],
             )
 
-        for i in range(LEAD):
+        for i in range(6):
             multiply_one(i, 1)
         quantise_o(0, 0)
         quantise_o(1, 0)
@@ -215,15 +215,11 @@ def tile_retentionmechanism_pb_kernel(tc, ao, w_qkv, out_w, tao, out):
         quantise_o(0, 1)
         quantise_o(1, 1)
         quantise_n(1)
-        for k in range(3):
-            quantise_w(9 + k)
-            quantise_n(2 + 2 * k)
-            quantise_n(3 + 2 * k)
 
         tabs = keep.tile([P, 1], F32)
         nc.scalar.activation(out=tabs[:], in_=tao_sb[:], func=ACT.Abs)
 
-        z = big.tile([P, RT, E], F32, tag="big", align_bytes=256)
+        z = big.tile([P, RT, E], F32, tag="z", align_bytes=256)
 
         def multiply_two(k):
             multiply_two_part(k // 2, 512 * (k % 2), 512, k)
@@ -249,16 +245,20 @@ def tile_retentionmechanism_pb_kernel(tc, ao, w_qkv, out_w, tao, out):
         def square_sum(i):
             nc.scalar.activation(out=junk_s[:], in_=z[:, i, :], func=ACT.Square, accum_out=stats[:, 1, i : i + 1])
 
+        ahead = [(i, 1) for i in range(6, LEAD)]
+        for i in range(LEAD, RT):
+            ahead += [(i, 0), (i, 1)]
         squared = 0
         for i in range(RT - 1):
-            if i % 3 == 0:
-                multiply_one(LEAD + i // 3, 0)
-                multiply_one(LEAD + i // 3, 1)
+            if ahead:
+                multiply_one(*ahead.pop(0))
             multiply_two(2 * i)
             multiply_two(2 * i + 1)
-            if i % 3 == 0:
-                quantise_n(LEAD + i // 3)
-            if i > 0:
+            if i + 2 < RT:
+                quantise_n(i + 2)
+            if LEAD + 1 + i < RT:
+                quantise_w(LEAD + 1 + i)
+            if i >= 1:
                 square_sum(squared)
                 squared += 1
         last = RT - 1

@@ -121,6 +121,12 @@ def tile_retentionmechanism_pb_kernel(tc, ao, w_qkv, out_w, tao, out):
 
         def transpose_w(i):
             xt = psum.tile([P, 4, P], F32, tag="bank", name="xt")
+            if i in (0, 4, 8):
+                source = ao_sb[:, 1, 0, 0, :] if i == 0 else w_sb[:, i - 1, :]
+                for k in range(4 if i == 0 else 3):
+                    nc.tensor.matmul(
+                        out=xt[:].rearrange("p b r -> p (b r)"), lhsT=source[:, 512 : 512 + P], rhs=source[:, 512:1024], start=True, stop=True
+                    )
             for b in range(4):
                 nc.tensor.transpose(xt[:, b, :], w_words[:, i, P * b : P * (b + 1)], ident[:])
             nc.scalar.copy(

from contextlib import ExitStack

import concourse.mybir as mybir
from concourse.masks import make_identity

F32 = mybir.dt.float32
BF16 = mybir.dt.bfloat16
U32 = mybir.dt.uint32
U8 = mybir.dt.uint8
FP8X4 = mybir.dt.float8_e4m3fn_x4
ALU = mybir.AluOpType
ACT = mybir.ActivationFunctionType
AX = mybir.AxisListType

P = 128
E = 1024
R = 1536
RT = R // P
FT = E // P
EPS_RMS = 1.1920929e-07
COUNT = R * E
LEAD = 8

FLOPS = 2 * 2 * R * E * E


def tile_retentionmechanism_pb_kernel(tc, ao, w_qkv, out_w, tao, out):
    nc = tc.nc
    with ExitStack() as ctx:
        keep = ctx.enter_context(tc.tile_pool(name="keep", bufs=1))
        big = ctx.enter_context(tc.tile_pool(name="big", bufs=1))
        swap = ctx.enter_context(tc.tile_pool(name="swap", bufs=1))
        psum = ctx.enter_context(tc.psum_pool(name="psum", bufs=8))
        ctx.enter_context(tc.manual_schedule())

        ident = keep.tile([P, P], F32)
        make_identity(nc, ident[:])
        ones = keep.tile([P, P], F32)
        nc.vector.memset(ones[:], 1.0)
        warm = keep.tile([P, 1], F32)
        nc.vector.memset(warm[:], 1.0)
        stats = keep.tile([P, 2, 32], F32)
        nc.vector.memset(stats[:], 0.0)

        warm_out = keep.tile([P, 1], F32)
        nc.scalar.activation(out=warm_out[:], in_=warm[:], func=ACT.Abs_reciprocal_sqrt)

        ao_sb = swap.tile([P, 2, 2, 2, E], BF16, tag="swap", align_bytes=256)
        ao_v = ao.rearrange("(c u p q) e -> c u p (q e)", c=2, u=2, q=2)
        for c in range(2):
            for u in range(2):
                if c == 0 and u == 0:
                    for q in range(2):
                        nc.sync.dma_start(out=ao_sb[:, c, u, q], in_=ao_v[c, u, :, q * E : (q + 1) * E])
                else:
                    nc.sync.dma_start(out=ao_sb[:, c, u].rearrange("p q e -> p (q e)"), in_=ao_v[c, u])
        w_sb = keep.tile([P, RT, E], BF16)
        w_v = w_qkv.rearrange("(p i) d -> p i d", i=RT)
        for i in range(0, RT, 2):
            nc.sync.dma_start(out=w_sb[:, i : i + 2, :], in_=w_v[:, i : i + 2, :])
        ow_sb = keep.tile([P, FT, E], BF16)
        ow_v = out_w.rearrange("(h p) e -> p h e", p=P)
        nc.sync.dma_start(out=ow_sb[:, 0:4, :], in_=ow_v[:, 0:4, :])
        nc.sync.dma_start(out=ow_sb[:, 4:8, :], in_=ow_v[:, 4:8, :])
        tao_sb = keep.tile([P, 1], BF16)
        nc.sync.dma_start(out=tao_sb[:], in_=tao.partition_broadcast(P))

        early = big.tile([P, (RT + 8) * E], BF16, tag="big", align_bytes=256)
        w_grouped = early[:, 0 : RT * E].rearrange("p (i x) -> p i x", i=RT)
        a_grouped = early[:, RT * E : (RT + 8) * E].rearrange("p (g c w j) -> p g c w j", g=2, c=2, j=4)
        a_codes = keep.tile([P, 2, 2, 512], U32, align_bytes=256)
        a_scales = keep.tile([P, 2, 2, 512], U8, align_bytes=256)
        w_codes = keep.tile([P, RT, 2, P], U32, align_bytes=256)
        w_scales = keep.tile([P, RT, 2, P], U8, align_bytes=256)
        o_codes = keep.tile([P, 2, E], U32, align_bytes=256)
        o_scales = keep.tile([P, 2, E], U8, align_bytes=256)
        n_grouped = keep.tile([P, RT, 2, P, 4], BF16, align_bytes=256)
        n_codes = keep.tile([P, RT, 2, P], U32, align_bytes=256)
        n_scales = keep.tile([P, RT, 2, P], U8, align_bytes=256)
        junk_v = keep.tile([P, E], BF16)
        junk_s = keep.tile([P, E], BF16)
        ss = keep.tile([P, 2, 4], F32)
        rstd = keep.tile([P, 2, 4], F32)
        w_words = w_sb[:].bitcast(F32)
        o_words = ow_sb[:].bitcast(F32)

        def sum_squares(c, u):
            nc.vector.scalar_tensor_tensor(
                out=junk_v[:], in0=ao_sb[:, c, u, 0, :], scalar=1.0, in1=ao_sb[:, c, u, 0, :],
                op0=ALU.mult, op1=ALU.mult, accum_out=ss[:, c, 2 * u : 2 * u + 1],
            )
            nc.scalar.activation(
                out=junk_s[:], in_=ao_sb[:, c, u, 1, :], func=ACT.Square, accum_out=ss[:, c, 2 * u + 1 : 2 * u + 2]
            )

        def inverse_rms(c):
            nc.scalar.activation(
                out=rstd[:, c, :], in_=ss[:, c, :], func=ACT.Abs_reciprocal_sqrt, scale=1.0 / E, bias=EPS_RMS
            )

        def scale_a(c, g):
            for j in range(4):
                part = ao_sb[:, c, j // 2, j % 2, 512 * g : 512 * (g + 1)]
                nc.vector.tensor_scalar(out=part, in0=part, scalar1=rstd[:, c, j : j + 1], scalar2=None, op0=ALU.mult)

        def regroup_a(g, c):
            rows = ao_sb[:, c].rearrange("p u q e -> p (u q) e")
            for v in range(2):
                first = 512 * g + 256 * v
                nc.vector.tensor_copy(
                    out=a_grouped[:, g, c, 256 * v : 256 * (v + 1), :].rearrange("p (s k m) j -> p k j m s", s=2, m=2),
                    in_=rows[:, :, first : first + 256].rearrange("p j (k m s) -> p k j m s", m=2, s=2),
                )

        def quantise_a(g):
            nc.vector.quantize_mx(
                out=a_codes[:, g].rearrange("p c w -> p (c w)").bitcast(FP8X4),
                scales=a_scales[:, g].rearrange("p c w -> p (c w)"),
                in_=a_grouped[:, g].rearrange("p c w j -> p (c w j)"),
            )

        def transpose_w(i):
            xt = psum.tile([P, 4, P], F32, tag="bank", name="xt")
            if i in (0, 4, 8):
                source = ao_sb[:, 1, 0, 0, :] if i == 0 else w_sb[:, i - 1, :]
                for k in range(4 if i == 0 else 3):
                    nc.tensor.matmul(
                        out=xt[:].rearrange("p b r -> p (b r)"), lhsT=source[:, 512 : 512 + P], rhs=source[:, 512:1024], start=True, stop=True
                    )
            for b in range(4):
                nc.tensor.transpose(xt[:, b, :], w_words[:, i, P * b : P * (b + 1)], ident[:])
            nc.scalar.copy(
                out=w_grouped[:, i, :].bitcast(F32).rearrange("p (c r u) -> p c r u", c=2, u=2),
                in_=xt[:].rearrange("p (c u) r -> p c r u", c=2),
            )

        def quantise_w(i):
            nc.vector.quantize_mx(
                out=w_codes[:, i].rearrange("p c r -> p (c r)").bitcast(FP8X4),
                scales=w_scales[:, i].rearrange("p c r -> p (c r)"),
                in_=w_grouped[:, i, :],
            )

        def multiply_one(i, g):
            acc = psum.tile([P, 4, P], F32, tag="bank", name="acc1")
            for t in range(4):
                for c in range(2):
                    nc.tensor.matmul_mx(
                        out=acc[:, t, :],
                        lhsT=a_codes[:, g, c, P * t : P * (t + 1)].bitcast(FP8X4),
                        lhsT_scale=a_scales[:, g, c, P * t : P * (t + 1)],
                        rhs=w_codes[:, i, c, :].bitcast(FP8X4),
                        rhs_scale=w_scales[:, i, c, :],
                        start=(c == 0),
                        stop=(c == 1),
                    )
            nc.scalar.activation(out=n_grouped[:, i, g], in_=acc[:].rearrange("p t r -> p r t"), func=ACT.Silu)

        def quantise_n(i):
            nc.vector.quantize_mx(
                out=n_codes[:, i].rearrange("p g r -> p (g r)").bitcast(FP8X4),
                scales=n_scales[:, i].rearrange("p g r -> p (g r)"),
                in_=n_grouped[:, i].rearrange("p g r t -> p (g r t)"),
            )

        sum_squares(0, 0)
        sum_squares(0, 1)
        sum_squares(1, 0)
        inverse_rms(0)
        sum_squares(1, 1)
        inverse_rms(1)
        nc.scalar.activation(out=warm_out[:], in_=warm[:], func=ACT.Silu)
        for i in range(LEAD + 2):
            transpose_w(i)
        scale_a(0, 0)
        scale_a(1, 0)
        regroup_a(0, 0)
        regroup_a(0, 1)
        quantise_w(0)
        quantise_a(0)
        for i in range(1, LEAD):
            quantise_w(i)

        scale_a(0, 1)
        scale_a(1, 1)
        regroup_a(1, 0)
        regroup_a(1, 1)
        quantise_w(8)
        quantise_a(1)

        for i in range(LEAD):
            multiply_one(i, 0)
        for i in range(LEAD + 2, RT):
            transpose_w(i)

        o_grouped = swap.tile([P, 2, 4 * E], BF16, tag="swap", align_bytes=256)
        o_grouped_words = o_grouped[:].bitcast(F32).rearrange("p g (f v) -> p g f v", v=2)
        for h in range(FT):
            xt = psum.tile([P, 4, P], F32, tag="bank", name="xt")
            for b in range(4):
                nc.tensor.transpose(xt[:, b, :], o_words[:, h, P * b : P * (b + 1)], ident[:])
            src = xt[:].rearrange("p (g v) f -> p g f v", g=2)
            dst = o_grouped_words[:, :, P * h : P * (h + 1), :]
            if h % 2 == 0:
                nc.vector.tensor_copy(out=dst, in_=src)
            else:
                nc.scalar.copy(out=dst, in_=src)

        def quantise_o(g, fh):
            nc.vector.quantize_mx(
                out=o_codes[:, g, 512 * fh : 512 * (fh + 1)].bitcast(FP8X4),
                scales=o_scales[:, g, 512 * fh : 512 * (fh + 1)],
                in_=o_grouped[:, g, 2048 * fh : 2048 * (fh + 1)],
            )

        for i in range(6):
            multiply_one(i, 1)
        quantise_o(0, 0)
        quantise_o(1, 0)
        quantise_n(0)
        quantise_o(0, 1)
        quantise_o(1, 1)
        quantise_n(1)

        tabs = keep.tile([P, 1], F32)
        nc.scalar.activation(out=tabs[:], in_=tao_sb[:], func=ACT.Abs)

        z = big.tile([P, RT, E], F32, tag="z", align_bytes=256)

        def multiply_two(k):
            multiply_two_part(k // 2, 512 * (k % 2), 512, k)

        def multiply_two_part(i, first, width, k):
            cols = slice(first, first + width)
            acc = psum.tile([P, width], F32, tag="bank", name="acc2")
            for g in range(2):
                nc.tensor.matmul_mx(
                    out=acc[:],
                    lhsT=n_codes[:, i, g, :].bitcast(FP8X4),
                    lhsT_scale=n_scales[:, i, g, :],
                    rhs=o_codes[:, g, cols].bitcast(FP8X4),
                    rhs_scale=o_scales[:, g, cols],
                    start=(g == 0),
                    stop=(g == 1),
                )
            nc.vector.scalar_tensor_tensor(
                out=z[:, i, cols], in0=acc[:], scalar=1.0, in1=w_sb[:, i, cols],
                op0=ALU.mult, op1=ALU.add, accum_out=stats[:, 0, k : k + 1],
            )

        def square_sum(i):
            nc.scalar.activation(out=junk_s[:], in_=z[:, i, :], func=ACT.Square, accum_out=stats[:, 1, i : i + 1])

        ahead = [(i, 1) for i in range(6, LEAD)]
        for i in range(LEAD, RT):
            ahead += [(i, 0), (i, 1)]
        squared = 0
        for i in range(RT - 1):
            if ahead:
                multiply_one(*ahead.pop(0))
            multiply_two(2 * i)
            multiply_two(2 * i + 1)
            if i + 2 < RT:
                quantise_n(i + 2)
            if LEAD + 1 + i < RT:
                quantise_w(LEAD + 1 + i)
            if i >= 1:
                square_sum(squared)
                squared += 1
        last = RT - 1
        multiply_two(2 * last)
        square_sum(squared)
        nc.scalar.activation(out=warm_out[:], in_=warm[:], func=ACT.Sqrt)
        multiply_two_part(last, 512, 256, 2 * last + 1)
        multiply_two_part(last, 768, 256, 2 * last + 2)

        idle = psum.tile([P, 512], F32, tag="bank", name="idle")
        for k in range(8):
            nc.tensor.matmul(out=idle[:], lhsT=w_sb[:, 0, 0:P], rhs=w_sb[:, 0, 0:512], start=True, stop=True)

        def square_sum_on_vector(first, width, out):
            part = z[:, last, first : first + width]
            nc.vector.scalar_tensor_tensor(
                out=junk_v[:, 0:width], in0=part, scalar=1.0, in1=part, op0=ALU.mult, op1=ALU.mult, accum_out=out
            )

        sums = keep.tile([P, 2], F32)
        last_square = keep.tile([P, 1], F32)
        square_sum_on_vector(0, 512, stats[:, 1, last : last + 1])
        nc.vector.tensor_reduce(out=sums[:, 0:1], in_=stats[:, 0, :], axis=AX.X, op=ALU.add)
        nc.vector.tensor_reduce(out=sums[:, 1:2], in_=stats[:, 1, :], axis=AX.X, op=ALU.add)
        square_sum_on_vector(512, 512, last_square[:])

        total = psum.tile([P, 1], F32, tag="bank", name="total")
        nc.tensor.matmul(out=total[:], lhsT=ones[:], rhs=sums[:, 0:1], start=True, stop=True)
        gate = keep.tile([P, 1], F32)
        nc.vector.tensor_scalar(out=gate[:], in0=tabs[:], scalar1=1e-08, scalar2=1.0, op0=ALU.max, op1=ALU.min)
        mean_part = keep.tile([P, 1], F32)
        nc.vector.tensor_scalar(
            out=mean_part[:], in0=total[:], scalar1=-1024.0 / COUNT / (COUNT - 1.0), scalar2=total[:, 0:1], op0=ALU.mult, op1=ALU.mult
        )
        total_sq = psum.tile([P, 1], F32, tag="bank", name="total_sq")
        nc.tensor.matmul(out=total_sq[:], lhsT=ones[:], rhs=sums[:, 1:2], start=True, stop=False)
        nc.tensor.matmul(out=total_sq[:], lhsT=ones[:], rhs=last_square[:], start=False, stop=True)
        root = keep.tile([P, 1], F32)
        nc.scalar.activation(out=root[:], in_=total_sq[:], func=ACT.Sqrt, scale=1024.0 / (COUNT - 1.0), bias=mean_part[:])
        den = keep.tile([P, 1], F32)
        nc.vector.tensor_scalar(out=den[:], in0=root[:], scalar1=32.0 * 1e-08, scalar2=None, op0=ALU.add)
        inv = keep.tile([P, 1], F32)
        nc.vector.reciprocal(out=inv[:], in_=den[:])

        out_v = out.rearrange("(p i) f -> p i f", i=RT)

        def scale_and_store(i, cols, queue):
            nc.vector.tensor_scalar(
                out=z[:, i, cols], in0=z[:, i, cols], scalar1=inv[:, 0:1], scalar2=gate[:, 0:1], op0=ALU.mult, op1=ALU.mult
            )
            queue.dma_start(out=out_v[:, i, cols], in_=z[:, i, cols])

        for k in range(4):
            scale_and_store(0, slice(256 * k, 256 * (k + 1)), nc.sync if k % 2 == 0 else nc.scalar)
        for i in range(1, RT):
            scale_and_store(i, slice(0, 1024), nc.sync if i % 2 == 1 else nc.scalar)
